import numpy as np
import ml_dtypes

BF16 = ml_dtypes.bfloat16


def bf(x):
    return np.asarray(x, np.float32).astype(BF16)


def f32(x):
    return np.asarray(x, np.float32)


def f64(x):
    return np.asarray(x).astype(np.float64)


def striped(idx):
    return np.tile(idx.reshape(-1, 16).T, (8, 1))


D, S, N, M, T = 128, 2048, 2048, 256, 4


def setup_inputs():
    return {"x": bf(np.random.standard_normal((D, S))), "w": bf(np.random.standard_normal((D, M)) / np.sqrt(D)), "b": f32(0.2 * np.random.standard_normal((M, 1))), "offs": striped(np.random.permutation(S)[:N])}


def reference(x, w, b, offs):
    idx = offs[:16].T.reshape(-1)
    h = f64(w).T @ f64(x)[:, idx] + f64(b)
    return h.reshape(M, N // T, T).max(axis=-1)

@@ -1,0 +1,59 @@
+import concourse.mybir as mybir
+
+BF16, F32, U16 = mybir.dt.bfloat16, mybir.dt.float32, mybir.dt.uint16
+
+P = 128
+NODES = 2048
+HALVES = 2
+PIECE = 512
+PIECES = NODES // PIECE
+GROUP = 4
+POOLED = PIECE // GROUP
+PER_COLUMN = 16
+
+FLOPS = 2 * P * HALVES * P * NODES
+
+
+def tile_graphnonlocal_kernel(tc, x, w, b, offs, out):
+    nc = tc.nc
+    out_by_half = out.rearrange("(h p) q -> p h q", p=P)
+
+    with (
+        tc.tile_pool(name="held", bufs=1) as held,
+        tc.tile_pool(name="work", bufs=PIECES) as work,
+        tc.psum_pool(name="psum", bufs=HALVES * PIECES) as psum,
+    ):
+        offsets = held.tile([P, NODES // PER_COLUMN], U16, name="offsets")
+        nodes = held.tile([P, NODES], BF16, name="nodes")
+        weights = held.tile([P, HALVES * P], BF16, name="weights")
+        bias = held.tile([P, HALVES], F32, name="bias")
+
+        nc.sync.dma_start(offsets[:], offs)
+        nc.scalar.dma_start(nodes[:], x)
+        nc.sync.dma_start(weights[:], w)
+        with nc.allow_non_contiguous_dma(reason="256 bias values, one to a partition and half"):
+            nc.gpsimd.dma_start(bias[:], b.rearrange("(h p) o -> p (h o)", p=P))
+
+        for piece in range(PIECES):
+            columns = PIECE // PER_COLUMN
+            looked_up = nodes[:].indirect(offsets[:, piece * columns : (piece + 1) * columns])
+            peaks = work.tile([P, HALVES, POOLED], F32, name="peaks")
+            pooled = work.tile([P, HALVES, POOLED], F32, name="pooled")
+            for half in range(HALVES):
+                product = psum.tile([P, PIECE], F32, name="product")
+                nc.tensor.matmul(
+                    product[:], weights[:, half * P : (half + 1) * P], looked_up, start=True, stop=True
+                )
+                nc.vector.tensor_reduce(
+                    peaks[:, half, :],
+                    product[:].rearrange("p (q t) -> p q t", t=GROUP),
+                    mybir.AxisListType.X,
+                    mybir.AluOpType.max,
+                )
+                nc.scalar.activation(
+                    pooled[:, half, :],
+                    peaks[:, half, :],
+                    mybir.ActivationFunctionType.Identity,
+                    bias=bias[:, half : half + 1],
+                )
+            nc.scalar.dma_start(out_by_half[:, :, piece * POOLED : (piece + 1) * POOLED], pooled[:])

@@ -10,6 +10,7 @@ PIECES = NODES // PIECE
 GROUP = 4
 POOLED = PIECE // GROUP
 PER_COLUMN = 16
+WARM_UPS = 8
 
 FLOPS = 2 * P * HALVES * P * NODES
 
@@ -21,7 +22,8 @@ def tile_graphnonlocal_kernel(tc, x, w, b, offs, out):
     with (
         tc.tile_pool(name="held", bufs=1) as held,
         tc.tile_pool(name="work", bufs=PIECES) as work,
-        tc.psum_pool(name="psum", bufs=HALVES * PIECES) as psum,
+        tc.psum_pool(name="psum", bufs=6) as psum,
+        tc.psum_pool(name="spare", bufs=1) as spare,
     ):
         offsets = held.tile([P, NODES // PER_COLUMN], U16, name="offsets")
         nodes = held.tile([P, NODES], BF16, name="nodes")
@@ -33,6 +35,12 @@ def tile_graphnonlocal_kernel(tc, x, w, b, offs, out):
         nc.sync.dma_start(weights[:], w)
         with nc.allow_non_contiguous_dma(reason="256 bias values, one to a partition and half"):
             nc.gpsimd.dma_start(bias[:], b.rearrange("(h p) o -> p (h o)", p=P))
+
+        zeros = held.tile([P, PIECE], BF16, name="zeros")
+        nc.vector.memset(zeros[:], 0.0)
+        unread = spare.tile([P, PIECE], F32, name="unread")
+        for repeat in range(WARM_UPS):
+            nc.tensor.matmul(unread[:], zeros[:, 0:P], zeros[:], start=True, stop=True)
 
         for piece in range(PIECES):
             columns = PIECE // PER_COLUMN

@@ -10,7 +10,6 @@ PIECES = NODES // PIECE
 GROUP = 4
 POOLED = PIECE // GROUP
 PER_COLUMN = 16
-WARM_UPS = 8
 
 FLOPS = 2 * P * HALVES * P * NODES
 
@@ -22,8 +21,7 @@ def tile_graphnonlocal_kernel(tc, x, w, b, offs, out):
     with (
         tc.tile_pool(name="held", bufs=1) as held,
         tc.tile_pool(name="work", bufs=PIECES) as work,
-        tc.psum_pool(name="psum", bufs=6) as psum,
-        tc.psum_pool(name="spare", bufs=1) as spare,
+        tc.psum_pool(name="psum", bufs=HALVES * PIECES) as psum,
     ):
         offsets = held.tile([P, NODES // PER_COLUMN], U16, name="offsets")
         nodes = held.tile([P, NODES], BF16, name="nodes")
@@ -36,32 +34,24 @@ def tile_graphnonlocal_kernel(tc, x, w, b, offs, out):
         with nc.allow_non_contiguous_dma(reason="256 bias values, one to a partition and half"):
             nc.gpsimd.dma_start(bias[:], b.rearrange("(h p) o -> p (h o)", p=P))
 
-        zeros = held.tile([P, PIECE], BF16, name="zeros")
-        nc.vector.memset(zeros[:], 0.0)
-        unread = spare.tile([P, PIECE], F32, name="unread")
-        for repeat in range(WARM_UPS):
-            nc.tensor.matmul(unread[:], zeros[:, 0:P], zeros[:], start=True, stop=True)
-
         for piece in range(PIECES):
             columns = PIECE // PER_COLUMN
             looked_up = nodes[:].indirect(offsets[:, piece * columns : (piece + 1) * columns])
-            peaks = work.tile([P, HALVES, POOLED], F32, name="peaks")
             pooled = work.tile([P, HALVES, POOLED], F32, name="pooled")
             for half in range(HALVES):
                 product = psum.tile([P, PIECE], F32, name="product")
                 nc.tensor.matmul(
                     product[:], weights[:, half * P : (half + 1) * P], looked_up, start=True, stop=True
                 )
-                nc.vector.tensor_reduce(
-                    peaks[:, half, :],
-                    product[:].rearrange("p (q t) -> p q t", t=GROUP),
-                    mybir.AxisListType.X,
-                    mybir.AluOpType.max,
-                )
+                groups = product[:].rearrange("p (q t) -> p q t", t=GROUP)
+                shift = bias[:, half : half + 1]
+                back = work.tile([P, POOLED, GROUP // 2], F32, name="back")
                 nc.scalar.activation(
-                    pooled[:, half, :],
-                    peaks[:, half, :],
-                    mybir.ActivationFunctionType.Identity,
-                    bias=bias[:, half : half + 1],
+                    back[:], groups[:, :, GROUP // 2 : GROUP], mybir.ActivationFunctionType.Identity, bias=shift
                 )
-            nc.scalar.dma_start(out_by_half[:, :, piece * POOLED : (piece + 1) * POOLED], pooled[:])
+                pairs = work.tile([P, POOLED, GROUP // 2], F32, name="pairs")
+                nc.vector.scalar_tensor_tensor(
+                    pairs[:], groups[:, :, 0 : GROUP // 2], shift, back[:], mybir.AluOpType.add, mybir.AluOpType.max
+                )
+                nc.vector.tensor_max(pooled[:, half, :], pairs[:, :, 0], pairs[:, :, 1])
+            nc.sync.dma_start(out_by_half[:, :, piece * POOLED : (piece + 1) * POOLED], pooled[:])

@@ -10,6 +10,7 @@ PIECES = NODES // PIECE
 GROUP = 4
 POOLED = PIECE // GROUP
 PER_COLUMN = 16
+WARM_UPS = 4
 
 FLOPS = 2 * P * HALVES * P * NODES
 
@@ -21,7 +22,8 @@ def tile_graphnonlocal_kernel(tc, x, w, b, offs, out):
     with (
         tc.tile_pool(name="held", bufs=1) as held,
         tc.tile_pool(name="work", bufs=PIECES) as work,
-        tc.psum_pool(name="psum", bufs=HALVES * PIECES) as psum,
+        tc.psum_pool(name="psum", bufs=6) as psum,
+        tc.psum_pool(name="spare", bufs=1) as spare,
     ):
         offsets = held.tile([P, NODES // PER_COLUMN], U16, name="offsets")
         nodes = held.tile([P, NODES], BF16, name="nodes")
@@ -34,24 +36,32 @@ def tile_graphnonlocal_kernel(tc, x, w, b, offs, out):
         with nc.allow_non_contiguous_dma(reason="256 bias values, one to a partition and half"):
             nc.gpsimd.dma_start(bias[:], b.rearrange("(h p) o -> p (h o)", p=P))
 
+        zeros = held.tile([P, PIECE], BF16, name="zeros")
+        nc.vector.memset(zeros[:], 0.0)
+        unread = spare.tile([P, PIECE], F32, name="unread")
+        for repeat in range(WARM_UPS):
+            nc.tensor.matmul(unread[:], zeros[:, 0:P], zeros[:], start=True, stop=True)
+
         for piece in range(PIECES):
             columns = PIECE // PER_COLUMN
             looked_up = nodes[:].indirect(offsets[:, piece * columns : (piece + 1) * columns])
+            peaks = work.tile([P, HALVES, POOLED], F32, name="peaks")
             pooled = work.tile([P, HALVES, POOLED], F32, name="pooled")
             for half in range(HALVES):
                 product = psum.tile([P, PIECE], F32, name="product")
                 nc.tensor.matmul(
                     product[:], weights[:, half * P : (half + 1) * P], looked_up, start=True, stop=True
                 )
-                groups = product[:].rearrange("p (q t) -> p q t", t=GROUP)
-                shift = bias[:, half : half + 1]
-                back = work.tile([P, POOLED, GROUP // 2], F32, name="back")
+                nc.vector.tensor_reduce(
+                    peaks[:, half, :],
+                    product[:].rearrange("p (q t) -> p q t", t=GROUP),
+                    mybir.AxisListType.X,
+                    mybir.AluOpType.max,
+                )
                 nc.scalar.activation(
-                    back[:], groups[:, :, GROUP // 2 : GROUP], mybir.ActivationFunctionType.Identity, bias=shift
+                    pooled[:, half, :],
+                    peaks[:, half, :],
+                    mybir.ActivationFunctionType.Identity,
+                    bias=bias[:, half : half + 1],
                 )
-                pairs = work.tile([P, POOLED, GROUP // 2], F32, name="pairs")
-                nc.vector.scalar_tensor_tensor(
-                    pairs[:], groups[:, :, 0 : GROUP // 2], shift, back[:], mybir.AluOpType.add, mybir.AluOpType.max
-                )
-                nc.vector.tensor_max(pooled[:, half, :], pairs[:, :, 0], pairs[:, :, 1])
-            nc.sync.dma_start(out_by_half[:, :, piece * POOLED : (piece + 1) * POOLED], pooled[:])
+            nc.scalar.dma_start(out_by_half[:, :, piece * POOLED : (piece + 1) * POOLED], pooled[:])

@@ -10,7 +10,6 @@ PIECES = NODES // PIECE
 GROUP = 4
 POOLED = PIECE // GROUP
 PER_COLUMN = 16
-WARM_UPS = 4
 
 FLOPS = 2 * P * HALVES * P * NODES
 
@@ -22,8 +21,7 @@ def tile_graphnonlocal_kernel(tc, x, w, b, offs, out):
     with (
         tc.tile_pool(name="held", bufs=1) as held,
         tc.tile_pool(name="work", bufs=PIECES) as work,
-        tc.psum_pool(name="psum", bufs=6) as psum,
-        tc.psum_pool(name="spare", bufs=1) as spare,
+        tc.psum_pool(name="psum", bufs=HALVES * PIECES) as psum,
     ):
         offsets = held.tile([P, NODES // PER_COLUMN], U16, name="offsets")
         nodes = held.tile([P, NODES], BF16, name="nodes")
@@ -34,13 +32,7 @@ def tile_graphnonlocal_kernel(tc, x, w, b, offs, out):
         nc.scalar.dma_start(nodes[:], x)
         nc.sync.dma_start(weights[:], w)
         with nc.allow_non_contiguous_dma(reason="256 bias values, one to a partition and half"):
-            nc.gpsimd.dma_start(bias[:], b.rearrange("(h p) o -> p (h o)", p=P))
-
-        zeros = held.tile([P, PIECE], BF16, name="zeros")
-        nc.vector.memset(zeros[:], 0.0)
-        unread = spare.tile([P, PIECE], F32, name="unread")
-        for repeat in range(WARM_UPS):
-            nc.tensor.matmul(unread[:], zeros[:, 0:P], zeros[:], start=True, stop=True)
+            nc.scalar.dma_start(bias[:], b.rearrange("(h p) o -> p (h o)", p=P))
 
         for piece in range(PIECES):
             columns = PIECE // PER_COLUMN

@@ -5,10 +5,8 @@ BF16, F32, U16 = mybir.dt.bfloat16, mybir.dt.float32, mybir.dt.uint16
 P = 128
 NODES = 2048
 HALVES = 2
-PIECE = 512
-PIECES = NODES // PIECE
+PIECES = (512, 512, 512, 256, 256)
 GROUP = 4
-POOLED = PIECE // GROUP
 PER_COLUMN = 16
 
 FLOPS = 2 * P * HALVES * P * NODES
@@ -20,8 +18,8 @@ def tile_graphnonlocal_kernel(tc, x, w, b, offs, out):
 
     with (
         tc.tile_pool(name="held", bufs=1) as held,
-        tc.tile_pool(name="work", bufs=PIECES) as work,
-        tc.psum_pool(name="psum", bufs=HALVES * PIECES) as psum,
+        tc.tile_pool(name="work", bufs=4) as work,
+        tc.psum_pool(name="psum", bufs=8) as psum,
     ):
         offsets = held.tile([P, NODES // PER_COLUMN], U16, name="offsets")
         nodes = held.tile([P, NODES], BF16, name="nodes")
@@ -34,13 +32,15 @@ def tile_graphnonlocal_kernel(tc, x, w, b, offs, out):
         with nc.allow_non_contiguous_dma(reason="256 bias values, one to a partition and half"):
             nc.scalar.dma_start(bias[:], b.rearrange("(h p) o -> p (h o)", p=P))
 
-        for piece in range(PIECES):
-            columns = PIECE // PER_COLUMN
-            looked_up = nodes[:].indirect(offsets[:, piece * columns : (piece + 1) * columns])
-            peaks = work.tile([P, HALVES, POOLED], F32, name="peaks")
-            pooled = work.tile([P, HALVES, POOLED], F32, name="pooled")
+        first = 0
+        for entries in PIECES:
+            looked_up = nodes[:].indirect(offsets[:, first // PER_COLUMN : (first + entries) // PER_COLUMN])
+            width = entries // GROUP
+            left = first // GROUP
+            peaks = work.tile([P, HALVES, width], F32, name="peaks")
+            pooled = work.tile([P, HALVES, width], F32, name="pooled")
             for half in range(HALVES):
-                product = psum.tile([P, PIECE], F32, name="product")
+                product = psum.tile([P, entries], F32, name="product")
                 nc.tensor.matmul(
                     product[:], weights[:, half * P : (half + 1) * P], looked_up, start=True, stop=True
                 )
@@ -56,4 +56,5 @@ def tile_graphnonlocal_kernel(tc, x, w, b, offs, out):
                     mybir.ActivationFunctionType.Identity,
                     bias=bias[:, half : half + 1],
                 )
-            nc.scalar.dma_start(out_by_half[:, :, piece * POOLED : (piece + 1) * POOLED], pooled[:])
+            nc.sync.dma_start(out_by_half[:, :, left : left + width], pooled[:])
+            first += entries

@@ -5,8 +5,10 @@ BF16, F32, U16 = mybir.dt.bfloat16, mybir.dt.float32, mybir.dt.uint16
 P = 128
 NODES = 2048
 HALVES = 2
-PIECES = (512, 512, 512, 256, 256)
+PIECE = 512
+PIECES = NODES // PIECE
 GROUP = 4
+POOLED = PIECE // GROUP
 PER_COLUMN = 16
 
 FLOPS = 2 * P * HALVES * P * NODES
@@ -18,8 +20,8 @@ def tile_graphnonlocal_kernel(tc, x, w, b, offs, out):
 
     with (
         tc.tile_pool(name="held", bufs=1) as held,
-        tc.tile_pool(name="work", bufs=4) as work,
-        tc.psum_pool(name="psum", bufs=8) as psum,
+        tc.tile_pool(name="work", bufs=PIECES) as work,
+        tc.psum_pool(name="psum", bufs=HALVES * PIECES) as psum,
     ):
         offsets = held.tile([P, NODES // PER_COLUMN], U16, name="offsets")
         nodes = held.tile([P, NODES], BF16, name="nodes")
@@ -32,15 +34,13 @@ def tile_graphnonlocal_kernel(tc, x, w, b, offs, out):
         with nc.allow_non_contiguous_dma(reason="256 bias values, one to a partition and half"):
             nc.scalar.dma_start(bias[:], b.rearrange("(h p) o -> p (h o)", p=P))
 
-        first = 0
-        for entries in PIECES:
-            looked_up = nodes[:].indirect(offsets[:, first // PER_COLUMN : (first + entries) // PER_COLUMN])
-            width = entries // GROUP
-            left = first // GROUP
-            peaks = work.tile([P, HALVES, width], F32, name="peaks")
-            pooled = work.tile([P, HALVES, width], F32, name="pooled")
+        for piece in range(PIECES):
+            columns = PIECE // PER_COLUMN
+            looked_up = nodes[:].indirect(offsets[:, piece * columns : (piece + 1) * columns])
+            peaks = work.tile([P, HALVES, POOLED], F32, name="peaks")
+            pooled = work.tile([P, HALVES, POOLED], F32, name="pooled")
             for half in range(HALVES):
-                product = psum.tile([P, entries], F32, name="product")
+                product = psum.tile([P, PIECE], F32, name="product")
                 nc.tensor.matmul(
                     product[:], weights[:, half * P : (half + 1) * P], looked_up, start=True, stop=True
                 )
@@ -56,5 +56,4 @@ def tile_graphnonlocal_kernel(tc, x, w, b, offs, out):
                     mybir.ActivationFunctionType.Identity,
                     bias=bias[:, half : half + 1],
                 )
-            nc.sync.dma_start(out_by_half[:, :, left : left + width], pooled[:])
-            first += entries
+            nc.sync.dma_start(out_by_half[:, :, piece * POOLED : (piece + 1) * POOLED], pooled[:])

@@ -5,7 +5,8 @@ BF16, F32, U16 = mybir.dt.bfloat16, mybir.dt.float32, mybir.dt.uint16
 P = 128
 NODES = 2048
 HALVES = 2
-PIECE = 512
+BANK = 512
+PIECE = 256
 PIECES = NODES // PIECE
 GROUP = 4
 POOLED = PIECE // GROUP
@@ -21,7 +22,7 @@ def tile_graphnonlocal_kernel(tc, x, w, b, offs, out):
     with (
         tc.tile_pool(name="held", bufs=1) as held,
         tc.tile_pool(name="work", bufs=PIECES) as work,
-        tc.psum_pool(name="psum", bufs=HALVES * PIECES) as psum,
+        tc.psum_pool(name="psum", bufs=8) as psum,
     ):
         offsets = held.tile([P, NODES // PER_COLUMN], U16, name="offsets")
         nodes = held.tile([P, NODES], BF16, name="nodes")
@@ -40,13 +41,13 @@ def tile_graphnonlocal_kernel(tc, x, w, b, offs, out):
             peaks = work.tile([P, HALVES, POOLED], F32, name="peaks")
             pooled = work.tile([P, HALVES, POOLED], F32, name="pooled")
             for half in range(HALVES):
-                product = psum.tile([P, PIECE], F32, name="product")
+                product = psum.tile([P, BANK], F32, name="product")
                 nc.tensor.matmul(
-                    product[:], weights[:, half * P : (half + 1) * P], looked_up, start=True, stop=True
+                    product[:, :PIECE], weights[:, half * P : (half + 1) * P], looked_up, start=True, stop=True
                 )
                 nc.vector.tensor_reduce(
                     peaks[:, half, :],
-                    product[:].rearrange("p (q t) -> p q t", t=GROUP),
+                    product[:, :PIECE].rearrange("p (q t) -> p q t", t=GROUP),
                     mybir.AxisListType.X,
                     mybir.AluOpType.max,
                 )

@@ -6,10 +6,9 @@ P = 128
 NODES = 2048
 HALVES = 2
 BANK = 512
-PIECE = 256
-PIECES = NODES // PIECE
+WIDTHS = [128] + [288] * 6 + [192]
+PIECES = len(WIDTHS)
 GROUP = 4
-POOLED = PIECE // GROUP
 PER_COLUMN = 16
 
 FLOPS = 2 * P * HALVES * P * NODES
@@ -35,26 +34,27 @@ def tile_graphnonlocal_kernel(tc, x, w, b, offs, out):
         with nc.allow_non_contiguous_dma(reason="256 bias values, one to a partition and half"):
             nc.scalar.dma_start(bias[:], b.rearrange("(h p) o -> p (h o)", p=P))
 
-        for piece in range(PIECES):
-            columns = PIECE // PER_COLUMN
-            looked_up = nodes[:].indirect(offsets[:, piece * columns : (piece + 1) * columns])
-            peaks = work.tile([P, HALVES, POOLED], F32, name="peaks")
-            pooled = work.tile([P, HALVES, POOLED], F32, name="pooled")
+        start = 0
+        for width in WIDTHS:
+            looked_up = nodes[:].indirect(offsets[:, start // PER_COLUMN : (start + width) // PER_COLUMN])
+            peaks = work.tile([P, HALVES, max(WIDTHS) // GROUP], F32, name="peaks")
+            pooled = work.tile([P, HALVES, width // GROUP], F32, name="pooled", tag=f"pooled{width}")
             for half in range(HALVES):
                 product = psum.tile([P, BANK], F32, name="product")
                 nc.tensor.matmul(
-                    product[:, :PIECE], weights[:, half * P : (half + 1) * P], looked_up, start=True, stop=True
+                    product[:, :width], weights[:, half * P : (half + 1) * P], looked_up, start=True, stop=True
                 )
                 nc.vector.tensor_reduce(
-                    peaks[:, half, :],
-                    product[:, :PIECE].rearrange("p (q t) -> p q t", t=GROUP),
+                    peaks[:, half, : width // GROUP],
+                    product[:, :width].rearrange("p (q t) -> p q t", t=GROUP),
                     mybir.AxisListType.X,
                     mybir.AluOpType.max,
                 )
                 nc.scalar.activation(
                     pooled[:, half, :],
-                    peaks[:, half, :],
+                    peaks[:, half, : width // GROUP],
                     mybir.ActivationFunctionType.Identity,
                     bias=bias[:, half : half + 1],
                 )
-            nc.sync.dma_start(out_by_half[:, :, piece * POOLED : (piece + 1) * POOLED], pooled[:])
+            nc.sync.dma_start(out_by_half[:, :, start // GROUP : (start + width) // GROUP], pooled[:])
+            start += width

@@ -25,12 +25,15 @@ def tile_graphnonlocal_kernel(tc, x, w, b, offs, out):
     ):
         offsets = held.tile([P, NODES // PER_COLUMN], U16, name="offsets")
         nodes = held.tile([P, NODES], BF16, name="nodes")
-        weights = held.tile([P, HALVES * P], BF16, name="weights")
+        key_weights = held.tile([P, P], BF16, name="key_weights")
+        value_weights = held.tile([P, P], BF16, name="value_weights")
+        weights = (key_weights, value_weights)
         bias = held.tile([P, HALVES], F32, name="bias")
 
         nc.sync.dma_start(offsets[:], offs)
         nc.scalar.dma_start(nodes[:], x)
-        nc.sync.dma_start(weights[:], w)
+        nc.sync.dma_start(key_weights[:], w[:, :P])
+        nc.scalar.dma_start(value_weights[:], w[:, P:])
         with nc.allow_non_contiguous_dma(reason="256 bias values, one to a partition and half"):
             nc.scalar.dma_start(bias[:], b.rearrange("(h p) o -> p (h o)", p=P))
 
@@ -42,7 +45,7 @@ def tile_graphnonlocal_kernel(tc, x, w, b, offs, out):
             for half in range(HALVES):
                 product = psum.tile([P, BANK], F32, name="product")
                 nc.tensor.matmul(
-                    product[:, :width], weights[:, half * P : (half + 1) * P], looked_up, start=True, stop=True
+                    product[:, :width], weights[half][:], looked_up, start=True, stop=True
                 )
                 nc.vector.tensor_reduce(
                     peaks[:, half, : width // GROUP],

@@ -6,7 +6,7 @@ P = 128
 NODES = 2048
 HALVES = 2
 BANK = 512
-WIDTHS = [128] + [288] * 6 + [192]
+WIDTHS = [320, 288, 288, 256, 256, 224, 224, 192]
 PIECES = len(WIDTHS)
 GROUP = 4
 PER_COLUMN = 16

import concourse.mybir as mybir

BF16, F32, U16 = mybir.dt.bfloat16, mybir.dt.float32, mybir.dt.uint16

P = 128
NODES = 2048
HALVES = 2
BANK = 512
WIDTHS = [320, 288, 288, 256, 256, 224, 224, 192]
PIECES = len(WIDTHS)
GROUP = 4
PER_COLUMN = 16

FLOPS = 2 * P * HALVES * P * NODES


def tile_graphnonlocal_kernel(tc, x, w, b, offs, out):
    nc = tc.nc
    out_by_half = out.rearrange("(h p) q -> p h q", p=P)

    with (
        tc.tile_pool(name="held", bufs=1) as held,
        tc.tile_pool(name="work", bufs=PIECES) as work,
        tc.psum_pool(name="psum", bufs=8) as psum,
    ):
        offsets = held.tile([P, NODES // PER_COLUMN], U16, name="offsets")
        nodes = held.tile([P, NODES], BF16, name="nodes")
        key_weights = held.tile([P, P], BF16, name="key_weights")
        value_weights = held.tile([P, P], BF16, name="value_weights")
        weights = (key_weights, value_weights)
        bias = held.tile([P, HALVES], F32, name="bias")

        nc.sync.dma_start(offsets[:], offs)
        nc.scalar.dma_start(nodes[:], x)
        nc.sync.dma_start(key_weights[:], w[:, :P])
        nc.scalar.dma_start(value_weights[:], w[:, P:])
        with nc.allow_non_contiguous_dma(reason="256 bias values, one to a partition and half"):
            nc.scalar.dma_start(bias[:], b.rearrange("(h p) o -> p (h o)", p=P))

        start = 0
        for width in WIDTHS:
            looked_up = nodes[:].indirect(offsets[:, start // PER_COLUMN : (start + width) // PER_COLUMN])
            peaks = work.tile([P, HALVES, max(WIDTHS) // GROUP], F32, name="peaks")
            pooled = work.tile([P, HALVES, width // GROUP], F32, name="pooled", tag=f"pooled{width}")
            for half in range(HALVES):
                product = psum.tile([P, BANK], F32, name="product")
                nc.tensor.matmul(
                    product[:, :width], weights[half][:], looked_up, start=True, stop=True
                )
                nc.vector.tensor_reduce(
                    peaks[:, half, : width // GROUP],
                    product[:, :width].rearrange("p (q t) -> p q t", t=GROUP),
                    mybir.AxisListType.X,
                    mybir.AluOpType.max,
                )
                nc.scalar.activation(
                    pooled[:, half, :],
                    peaks[:, half, : width // GROUP],
                    mybir.ActivationFunctionType.Identity,
                    bias=bias[:, half : half + 1],
                )
            nc.sync.dma_start(out_by_half[:, :, start // GROUP : (start + width) // GROUP], pooled[:])
            start += width
